import numpy as np
import ml_dtypes


def mxq(x, axis, fmt="e4m3"):
    dtype, down = {"e4m3": (ml_dtypes.float8_e4m3fn, 7), "e5m2": (ml_dtypes.float8_e5m2, 14)}[fmt]
    v = np.moveaxis(np.asarray(x, np.float32).astype(ml_dtypes.bfloat16).astype(np.float64), axis, -1)
    blocks = v.reshape(v.shape[:-1] + (-1, 32))
    amax = np.abs(blocks).max(-1, keepdims=True)
    byte = np.maximum(np.where(amax > 0, np.frexp(amax)[1] - 1 + 127, 0) - down, 1)
    scale = np.exp2(byte - 127.0)
    codes = (blocks / scale).astype(np.float32).astype(dtype).astype(np.float64)
    return np.moveaxis((codes * scale).reshape(v.shape), -1, axis)


WIDE = False


def mx_kscale(k):
    if not WIDE:
        return np.ones(k)
    levels = np.array([10, -10, 5, -5, 0])
    a = np.random.permutation(np.resize(levels, k // 512 * 4)).reshape(k // 512, 4)
    idx = np.arange(k)
    return np.exp2(a[idx // 512, idx % 128 // 32])


BF16 = ml_dtypes.bfloat16


def bf(x):
    return np.asarray(x, np.float32).astype(BF16)


def f64(x):
    return np.asarray(x).astype(np.float64)


B, L, D, C = 128, 20, 512, 512
EPS = 1e-12


def conv_relu(xq, wq, b):
    k = wq.shape[0]
    n = xq.shape[1]
    out = b
    for j in range(k):
        out = out + (xq[:, j:n - k + 1 + j] @ wq[j])
    return np.maximum(out, 0.0)


def l2norm(x, axis):
    n = np.sqrt(np.sum(x * x, axis=axis, keepdims=True))
    return x / np.maximum(n, EPS)


def setup_inputs():
    s = mx_kscale(D)

    def wdraw(k):
        return bf(np.random.standard_normal((k, D, C)) / np.sqrt(k * D) / s[None, :, None])

    return {"words_emb": bf(np.random.standard_normal((B, L, D)) * s),
            "W1": wdraw(1), "b1": bf(np.random.standard_normal(C) * 0.3),
            "W2": wdraw(2), "b2": bf(np.random.standard_normal(C) * 0.3),
            "W3": wdraw(3), "b3": bf(np.random.standard_normal(C) * 0.3)}


def reference(words_emb, W1, b1, W2, b2, W3, b3):
    xq = mxq(f64(words_emb), 2, "e4m3")
    a = conv_relu(xq, mxq(f64(W1), 1, "e4m3"), f64(b1))
    b_ = conv_relu(xq, mxq(f64(W2), 1, "e4m3"), f64(b2))
    c = conv_relu(xq, mxq(f64(W3), 1, "e4m3"), f64(b3))
    b_pad = np.pad(b_, ((0, 0), (0, L - b_.shape[1]), (0, 0)))
    c_pad = np.pad(c, ((0, 0), (0, L - c.shape[1]), (0, 0)))
    code = np.maximum(np.maximum(a, b_pad), c_pad)
    code = l2norm(code, 2)
    words_out = np.transpose(code, (0, 2, 1))
    pooled = (a.max(axis=1) + b_.max(axis=1) + c.max(axis=1)) / 3.0
    return (words_out, pooled)

@@ -1,0 +1,368 @@
+from contextlib import ExitStack
+
+import concourse.mybir as mybir
+from concourse.masks import make_identity
+
+F32 = mybir.dt.float32
+BF16 = mybir.dt.bfloat16
+U32 = mybir.dt.uint32
+U8 = mybir.dt.uint8
+FP8X4 = mybir.dt.float8_e4m3fn_x4
+ALU = mybir.AluOpType
+ACT = mybir.ActivationFunctionType
+
+P = 128
+L = 20
+D = 512
+C = 512
+NH = 64
+HC = L * NH
+R = 4
+TAP0 = {1: 0, 2: 1, 3: 3}
+CH = ((0, 512, 0, 8), (512, 512, 8, 8), (1024, 256, 16, 4))
+LAG = 4
+EPS2 = 1.0e-24
+
+FLOPS = 2 * D * C * P * (20 + 2 * 19 + 3 * 18)
+
+
+def tile_bertheading_pa_kernel(tc, words_emb, W1, b1, W2, b2, W3, b3, out_0, out_1):
+    nc = tc.nc
+    with ExitStack() as ctx:
+        keep = ctx.enter_context(tc.tile_pool(name="keep", bufs=1))
+        main = ctx.enter_context(tc.tile_pool(name="main", bufs=2))
+        psum_y = ctx.enter_context(tc.psum_pool(name="psum_y", bufs=6))
+        psum_aux = ctx.enter_context(tc.psum_pool(name="psum_aux", bufs=2))
+
+        ident = keep.tile([P, P], F32, name="ident")
+        make_identity(nc, ident[:])
+
+        ones = keep.tile([P, P], F32, name="ones")
+        nc.vector.memset(ones[:], 1.0)
+        warm_in = keep.tile([P, 1], F32, name="warm_in")
+        warm_out = keep.tile([P, 1], F32, name="warm_out")
+        nc.vector.memset(warm_in[:], 1.0)
+        negeps = keep.tile([P, 1], F32, name="negeps")
+        nc.vector.memset(negeps[:], -EPS2)
+        poseps = keep.tile([P, 1], F32, name="poseps")
+        nc.vector.memset(poseps[:], EPS2)
+
+        bias = keep.tile([P, 3, R], F32, name="bias")
+        braws = []
+        for k, b in enumerate((b1, b2, b3)):
+            braw = keep.tile([P, R], BF16, name="braw%d" % k)
+            nc.scalar.dma_start(out=braw[:], in_=b.rearrange("(m r) -> m r", r=R))
+            braws.append(braw)
+        nc.scalar.activation(out=warm_out[:], in_=warm_in[:], func=ACT.Abs_reciprocal_sqrt)
+
+        xq = keep.tile([P, 2 * HC], U32, name="xq", align_bytes=64)
+        xs = keep.tile([P, 2 * HC], U8, name="xs", align_bytes=64)
+        wq = keep.tile([P, 6, C], U32, name="wq", align_bytes=64)
+        ws = keep.tile([P, 6, C], U8, name="ws", align_bytes=64)
+        pt = keep.tile([P, R, P], F32, name="pt")
+        pooled = keep.tile([P, C], F32, name="pooled")
+
+        half = {}
+        chunk = {}
+        for nb in range(2):
+            code_t = main.tile([P, R, HC], F32, tag="code", name="code")
+            pl_t = main.tile([P, 3 * R, 512], F32, tag="pl", name="pl")
+            half[nb] = (code_t, pl_t)
+
+        def conv_group(k, nb, r, p0, npos, bank=None):
+            n = npos * NH
+            y = bank
+            if bank is None:
+                y = psum_y.tile([P, 512], F32, tag="y", name="y")
+            for j in range(k):
+                tap = TAP0[k] + j
+                c0 = nb * HC + (p0 + j) * NH
+                nc.tensor.matmul_mx(
+                    out=y[:, :n],
+                    lhsT=wq[:, tap, r * P : (r + 1) * P].bitcast(FP8X4),
+                    lhsT_scale=ws[:, tap, r * P : (r + 1) * P],
+                    rhs=xq[:, c0 : c0 + n].bitcast(FP8X4),
+                    rhs_scale=xs[:, c0 : c0 + n],
+                    start=(j == 0),
+                    stop=(j == k - 1),
+                )
+            return y
+
+        def relu_out(dst, y, k, r):
+            nc.scalar.activation(out=dst, in_=y, func=ACT.Relu, bias=bias[:, k - 1, r : r + 1], scale=1.0)
+
+        def merge(dst, y, k, r):
+            nc.vector.scalar_tensor_tensor(
+                out=dst, in0=y, scalar=bias[:, k - 1, r : r + 1], in1=dst, op0=ALU.add, op1=ALU.max
+            )
+
+        def vmax(dst, a, b):
+            nc.vector.tensor_tensor(out=dst, in0=a, in1=b, op=ALU.max)
+
+        def k12(nb, r, ch):
+            code, pl = half[nb]
+            col0, t, p0, npos = CH[ch]
+            cd = code[:, r, col0 : col0 + t]
+            if ch == 0:
+                y1 = conv_group(1, nb, r, 0, 8)
+                y2 = conv_group(2, nb, r, 0, 8)
+                relu_out(pl[:, r, :], y1[:], 1, r)
+                relu_out(pl[:, R + r, :], y2[:], 2, r)
+                vmax(cd, pl[:, r, :], pl[:, R + r, :])
+            elif ch == 1:
+                y1 = conv_group(1, nb, r, 8, 8)
+                y2 = conv_group(2, nb, r, 8, 8)
+                relu_out(cd, y1[:], 1, r)
+                vmax(pl[:, r, :], pl[:, r, :], cd)
+                merge(cd, y2[:], 2, r)
+                merge(pl[:, R + r, :], y2[:], 2, r)
+            else:
+                y1 = conv_group(1, nb, r, 16, 4)
+                y2 = conv_group(2, nb, r, 15, 4)
+                relu_out(cd, y1[:, :256], 1, r)
+                vmax(pl[:, r, :256], pl[:, r, :256], cd)
+                merge(code[:, r, col0 : col0 + 192], y2[:, 64:256], 2, r)
+                merge(pl[:, R + r, :192], y2[:, 64:256], 2, r)
+
+        y3s = {}
+
+        def k3_code(nb, ch, r):
+            code, pl = half[nb]
+            col0, t, p0, npos = CH[ch]
+            cd = code[:, r, col0 : col0 + t]
+            if ch == 0:
+                y3 = conv_group(3, nb, r, 0, 8)
+                relu_out(pl[:, 2 * R + r, :], y3[:], 3, r)
+                vmax(cd, cd, pl[:, 2 * R + r, :])
+            elif ch == 1:
+                y3 = conv_group(3, nb, r, 8, 8)
+                merge(cd, y3[:], 3, r)
+                y3s[(nb, ch, r)] = y3[:]
+            else:
+                if r == 0:
+                    y3s[nb] = psum_y.tile([P, R, P], F32, tag="y", name="y3c")
+                y3 = y3s[nb][:, r, :]
+                conv_group(3, nb, r, 16, 2, bank=y3)
+                merge(code[:, r, col0 : col0 + 128], y3, 3, r)
+                y3s[(nb, ch, r)] = y3
+
+        def k3_pool(nb, ch, r):
+            pl = half[nb][1]
+            if ch == 1:
+                merge(pl[:, 2 * R + r, :], y3s[(nb, ch, r)], 3, r)
+            elif ch == 2:
+                merge(pl[:, 2 * R + r, :128], y3s[(nb, ch, r)], 3, r)
+
+        with tc.tile_pool(name="stage", bufs=1) as stage:
+            xraw = {}
+            wraw = {}
+            wgs = {}
+            taps = ((W1, 0), (W2, 0), (W2, 1), (W3, 0), (W3, 1), (W3, 2))
+
+            def load_x(i):
+                t = stage.tile([P, 4 * D], BF16, name="xraw%d" % i)
+                nc.sync.dma_start(out=t[:], in_=words_emb[:, 4 * i : 4 * i + 4, :].rearrange("n p d -> n (p d)"))
+                xraw[i] = t
+
+            def load_w(tap):
+                w, j = taps[tap]
+                t = stage.tile([P, 4, C], BF16, name="wraw%d" % tap)
+                nc.sync.dma_start(
+                    out=t[:].rearrange("q (u e) c -> q u e c", u=2),
+                    in_=w[j].rearrange("(u q e) c -> q u e c", u=2, e=2),
+                )
+                wraw[tap] = t
+
+            load_w(0)
+            load_x(0)
+            load_x(1)
+            load_w(1)
+            load_x(2)
+            load_w(2)
+            load_x(3)
+            load_x(4)
+            load_w(3)
+            load_w(4)
+            load_w(5)
+
+            xg = stage.tile([P, 2 * HC * 4], BF16, name="xg", align_bytes=64)
+            xg32 = xg[:].bitcast(F32)
+
+            def x_chunk(i):
+                xw = xraw[i][:].bitcast(F32)
+                for h in range(2):
+                    xt = psum_y.tile([P, 2, 2, P], F32, tag="y", name="xt")
+                    for pp in range(2):
+                        for u in range(2):
+                            w0 = (2 * h + pp) * 256 + u * 128
+                            nc.tensor.transpose(xt[:, pp, u, :], xw[:, w0 : w0 + 128], ident[:])
+                    pos = 4 * i + 2 * h
+                    for nb in range(2):
+                        f0 = (nb * HC + pos * NH) * 2
+                        dst = xg32[:, f0 : f0 + 256].rearrange("q (pp n u) -> q pp n u", pp=2, u=2)
+                        src = xt[:, :, :, nb * NH : (nb + 1) * NH].rearrange("q pp u n -> q pp n u")
+                        nc.scalar.copy(out=dst, in_=src)
+
+            def x_quant(c0, cols):
+                nc.vector.quantize_mx(
+                    out=xq[:, c0 : c0 + cols].bitcast(FP8X4),
+                    scales=xs[:, c0 : c0 + cols],
+                    in_=xg[:, 4 * c0 : 4 * (c0 + cols)],
+                )
+
+            def w_regroup(tap, on_vector):
+                wg = stage.tile([P, C, 4], BF16, tag="wg", name="wg", bufs=3, align_bytes=64)
+                dst = wg[:].rearrange("q (r m) t -> q r m t", r=R)
+                src = wraw[tap][:].rearrange("q t (m r) -> q r m t", r=R)
+                if on_vector:
+                    nc.vector.tensor_copy(out=dst, in_=src)
+                else:
+                    nc.scalar.copy(out=dst, in_=src)
+                wgs[tap] = wg
+
+            def w_quant(tap):
+                nc.vector.quantize_mx(
+                    out=wq[:, tap, :].bitcast(FP8X4),
+                    scales=ws[:, tap, :],
+                    in_=wgs[tap][:].rearrange("q c t -> q (c t)"),
+                )
+
+            w_regroup(0, True)
+            for k in range(3):
+                nc.vector.tensor_copy(out=bias[:, k, :], in_=braws[k][:])
+            x_chunk(0)
+            x_chunk(1)
+            w_quant(0)
+            w_regroup(1, True)
+            x_quant(0, 256)
+            w_quant(1)
+            x_chunk(2)
+            x_quant(256, 256)
+            w_regroup(2, True)
+            x_quant(512, 256)
+            w_quant(2)
+            k12(0, 0, 0)
+            x_chunk(3)
+            x_chunk(4)
+            x_quant(768, 256)
+            x_quant(1024, 256)
+            k12(0, 0, 1)
+            k12(0, 0, 2)
+            w_regroup(3, False)
+            for ch in range(3):
+                k12(0, 1, ch)
+            w_regroup(4, False)
+            w_quant(3)
+            for ch in range(3):
+                k12(0, 2, ch)
+            w_regroup(5, True)
+            w_quant(4)
+            for ch in range(3):
+                k12(0, 3, ch)
+            w_quant(5)
+            x_quant(HC, 1024)
+            x_quant(HC + 1024, 256)
+
+        late = ctx.enter_context(tc.tile_pool(name="late", bufs=2))
+        o0v = out_0.rearrange("n (m r) p -> m n (r p)", r=R)
+
+        def norm_part(nb, ch, r):
+            code = half[nb][0]
+            col0, t, p0, npos = CH[ch]
+            if r == 0:
+                sq_t = late.tile([P, R, 512], F32, tag="sq", name="sq")
+                ns_t = psum_aux.tile([P, 512], F32, tag="aux", name="ns")
+                chunk[(nb, ch)] = (sq_t, ns_t)
+            sq, ns = chunk[(nb, ch)]
+            nc.scalar.activation(out=sq[:, r, :t], in_=code[:, r, col0 : col0 + t], func=ACT.Square)
+            if r % 2 == 1:
+                nc.gpsimd.tensor_tensor(out=sq[:, r, :t], in0=sq[:, r, :t], in1=sq[:, r - 1, :t], op=ALU.add)
+                nc.tensor.matmul(out=ns[:, :t], lhsT=ones[:], rhs=sq[:, r, :t], start=(r == 1), stop=(r == R - 1))
+
+        def finish_chunk(nb, ch):
+            code = half[nb][0]
+            col0, t, p0, npos = CH[ch]
+            ns = chunk[(nb, ch)][1]
+            if ch == 0:
+                outa_t = late.tile([P, NH // 2, R * L], F32, tag="outa", name="outa")
+                outb_t = late.tile([P, NH // 2, R * L], F32, tag="outb", name="outb")
+                half[(nb, "out")] = (outa_t, outb_t)
+            rn = late.tile([P, 512], F32, tag="rn", name="rn")
+            nc.scalar.activation(
+                out=rn[:, :t].rearrange("m (n p) -> m n p", n=NH),
+                in_=ns[:, :t].rearrange("m (p n) -> m n p", n=NH),
+                func=ACT.Relu,
+                bias=negeps[:],
+                scale=1.0,
+            )
+            nc.scalar.activation(out=rn[:, :t], in_=rn[:, :t], func=ACT.Abs_reciprocal_sqrt, bias=poseps[:], scale=1.0)
+            pieces = 4 if ch == 2 else 2
+            w = NH // pieces
+            for q in range(pieces):
+                nsl = slice(q * w, (q + 1) * w)
+                part = (q * w) // (NH // 2)
+                outt = half[(nb, "out")][part]
+                osl = slice(q * w - part * (NH // 2), (q + 1) * w - part * (NH // 2))
+                eng = nc.vector if (nb == 1 and part == 0) else nc.gpsimd
+                eng.tensor_tensor(
+                    out=outt[:].rearrange("m n (r p) -> m n r p", r=R)[:, osl, :, p0 : p0 + npos],
+                    in0=code[:, :, col0 : col0 + t].rearrange("m r (p n) -> m n r p", n=NH)[:, nsl, :, :],
+                    in1=rn[:, :t]
+                    .rearrange("m (n p) -> m n p", n=NH)[:, nsl, :]
+                    .unsqueeze(2)
+                    .to_broadcast([P, w, R, npos]),
+                    op=ALU.mult,
+                )
+                if ch == 2:
+                    n0 = nb * NH + q * w
+                    nc.sync.dma_start(out=o0v[:, n0 : n0 + w, :], in_=outt[:, osl, :])
+
+        def trees(nb):
+            pl = half[nb][1]
+            for w in (256, 128, 64):
+                vmax(pl[:, :, :w], pl[:, :, :w], pl[:, :, w : 2 * w])
+            ph = pt[:, :, nb * NH : (nb + 1) * NH]
+            nc.vector.tensor_tensor(out=ph, in0=pl[:, 0:R, :NH], in1=pl[:, R : 2 * R, :NH], op=ALU.add)
+            nc.vector.tensor_tensor(out=ph, in0=ph, in1=pl[:, 2 * R : 3 * R, :NH], op=ALU.add)
+
+        items = [(3, 0, ch, r) for ch in range(3) for r in range(R)]
+        items += [(12, 1, r, ch) for r in range(R) for ch in range(3)]
+        items += [(3, 1, ch, r) for ch in range(3) for r in range(R)]
+        pending = []
+        n_items = len(items)
+        for i in range(n_items + LAG + 2):
+            if i < n_items:
+                kind, nb, a, b = items[i]
+                if kind == 12:
+                    k12(nb, a, b)
+                else:
+                    lag = LAG if nb == 0 else 2
+                    k3_code(nb, a, b)
+                    if nb == 0:
+                        k3_pool(nb, a, b)
+                    pending.append((i + lag, 0, nb, a, b))
+                    if b == R - 1:
+                        pending.append((i + lag + 1, 1, nb, a, b))
+            due = [e for e in pending if e[0] <= i]
+            pending = [e for e in pending if e[0] > i]
+            for e in due:
+                if e[1] == 0:
+                    norm_part(e[2], e[3], e[4])
+                else:
+                    finish_chunk(e[2], e[3])
+        for ch in (1, 2):
+            for r in range(R):
+                k3_pool(1, ch, r)
+        trees(0)
+        trees(1)
+
+        ptp = psum_aux.tile([P, R, P], F32, tag="aux", name="ptp")
+        for r in range(R):
+            nc.tensor.transpose(ptp[:, r, :], pt[:, r, :], ident[:])
+        nc.scalar.activation(
+            out=pooled[:].rearrange("n (m r) -> n m r", r=R),
+            in_=ptp[:].rearrange("n r m -> n m r"),
+            func=ACT.Copy,
+            scale=1.0 / 3.0,
+        )
+        nc.sync.dma_start(out=out_1, in_=pooled[:])

@@ -275,9 +275,7 @@ def tile_bertheading_pa_kernel(tc, words_emb, W1, b1, W2, b2, W3, b3, out_0, out
                 chunk[(nb, ch)] = (sq_t, ns_t)
             sq, ns = chunk[(nb, ch)]
             nc.scalar.activation(out=sq[:, r, :t], in_=code[:, r, col0 : col0 + t], func=ACT.Square)
-            if r % 2 == 1:
-                nc.gpsimd.tensor_tensor(out=sq[:, r, :t], in0=sq[:, r, :t], in1=sq[:, r - 1, :t], op=ALU.add)
-                nc.tensor.matmul(out=ns[:, :t], lhsT=ones[:], rhs=sq[:, r, :t], start=(r == 1), stop=(r == R - 1))
+            nc.tensor.matmul(out=ns[:, :t], lhsT=ones[:], rhs=sq[:, r, :t], start=(r == 0), stop=(r == R - 1))
 
         def finish_chunk(nb, ch):
             code = half[nb][0]
@@ -303,8 +301,7 @@ def tile_bertheading_pa_kernel(tc, words_emb, W1, b1, W2, b2, W3, b3, out_0, out
                 part = (q * w) // (NH // 2)
                 outt = half[(nb, "out")][part]
                 osl = slice(q * w - part * (NH // 2), (q + 1) * w - part * (NH // 2))
-                eng = nc.vector if (nb == 1 and part == 0) else nc.gpsimd
-                eng.tensor_tensor(
+                nc.vector.tensor_tensor(
                     out=outt[:].rearrange("m n (r p) -> m n r p", r=R)[:, osl, :, p0 : p0 + npos],
                     in0=code[:, :, col0 : col0 + t].rearrange("m r (p n) -> m n r p", n=NH)[:, nsl, :, :],
                     in1=rn[:, :t]

@@ -96,6 +96,12 @@ def tile_bertheading_pa_kernel(tc, words_emb, W1, b1, W2, b2, W3, b3, out_0, out
                 out=dst, in0=y, scalar=bias[:, k - 1, r : r + 1], in1=dst, op0=ALU.add, op1=ALU.max
             )
 
+        def bank_by_n(ap):
+            return ap.rearrange("m (p n) -> m n p", n=NH)
+
+        def by_n(ap):
+            return ap.rearrange("m (n p) -> m n p", n=NH)
+
         def vmax(dst, a, b):
             nc.vector.tensor_tensor(out=dst, in0=a, in1=b, op=ALU.max)
 
@@ -105,24 +111,34 @@ def tile_bertheading_pa_kernel(tc, words_emb, W1, b1, W2, b2, W3, b3, out_0, out
             cd = code[:, r, col0 : col0 + t]
             if ch == 0:
                 y1 = conv_group(1, nb, r, 0, 8)
+                y1d = conv_group(1, nb, r, 0, 8)
                 y2 = conv_group(2, nb, r, 0, 8)
-                relu_out(pl[:, r, :], y1[:], 1, r)
-                relu_out(pl[:, R + r, :], y2[:], 2, r)
-                vmax(cd, pl[:, r, :], pl[:, R + r, :])
+                relu_out(by_n(pl[:, r, :]), bank_by_n(y1[:]), 1, r)
+                relu_out(by_n(pl[:, R + r, :]), bank_by_n(y2[:]), 2, r)
+                nc.vector.scalar_tensor_tensor(
+                    out=by_n(cd),
+                    in0=bank_by_n(y1d[:]),
+                    scalar=bias[:, 0, r : r + 1],
+                    in1=by_n(pl[:, R + r, :]),
+                    op0=ALU.add,
+                    op1=ALU.max,
+                )
             elif ch == 1:
                 y1 = conv_group(1, nb, r, 8, 8)
+                y1d = conv_group(1, nb, r, 8, 8)
                 y2 = conv_group(2, nb, r, 8, 8)
-                relu_out(cd, y1[:], 1, r)
-                vmax(pl[:, r, :], pl[:, r, :], cd)
-                merge(cd, y2[:], 2, r)
-                merge(pl[:, R + r, :], y2[:], 2, r)
+                relu_out(by_n(cd), bank_by_n(y1[:]), 1, r)
+                merge(by_n(pl[:, r, :]), bank_by_n(y1d[:]), 1, r)
+                merge(by_n(cd), bank_by_n(y2[:]), 2, r)
+                merge(by_n(pl[:, R + r, :]), bank_by_n(y2[:]), 2, r)
             else:
                 y1 = conv_group(1, nb, r, 16, 4)
+                y1d = conv_group(1, nb, r, 16, 4)
                 y2 = conv_group(2, nb, r, 15, 4)
                 relu_out(cd, y1[:, :256], 1, r)
-                vmax(pl[:, r, :256], pl[:, r, :256], cd)
+                merge(by_n(pl[:, r, :])[:, :, 0:4], bank_by_n(y1d[:, :256]), 1, r)
                 merge(code[:, r, col0 : col0 + 192], y2[:, 64:256], 2, r)
-                merge(pl[:, R + r, :192], y2[:, 64:256], 2, r)
+                merge(by_n(pl[:, R + r, :])[:, :, 0:4], bank_by_n(y2[:, :256]), 2, r)
 
         y3s = {}
 
@@ -132,26 +148,26 @@ def tile_bertheading_pa_kernel(tc, words_emb, W1, b1, W2, b2, W3, b3, out_0, out
             cd = code[:, r, col0 : col0 + t]
             if ch == 0:
                 y3 = conv_group(3, nb, r, 0, 8)
-                relu_out(pl[:, 2 * R + r, :], y3[:], 3, r)
+                relu_out(by_n(pl[:, 2 * R + r, :]), bank_by_n(y3[:]), 3, r)
                 vmax(cd, cd, pl[:, 2 * R + r, :])
             elif ch == 1:
                 y3 = conv_group(3, nb, r, 8, 8)
-                merge(cd, y3[:], 3, r)
+                merge(by_n(cd), bank_by_n(y3[:]), 3, r)
                 y3s[(nb, ch, r)] = y3[:]
             else:
-                if r == 0:
-                    y3s[nb] = psum_y.tile([P, R, P], F32, tag="y", name="y3c")
-                y3 = y3s[nb][:, r, :]
-                conv_group(3, nb, r, 16, 2, bank=y3)
-                merge(code[:, r, col0 : col0 + 128], y3, 3, r)
+                if r % 2 == 0:
+                    y3s[nb] = psum_y.tile([P, 2, 256], F32, tag="y", name="y3c")
+                y3 = y3s[nb][:, r % 2, :]
+                conv_group(3, nb, r, 14, 4, bank=y3)
+                merge(code[:, r, col0 : col0 + 128], y3[:, 128:256], 3, r)
                 y3s[(nb, ch, r)] = y3
 
         def k3_pool(nb, ch, r):
             pl = half[nb][1]
             if ch == 1:
-                merge(pl[:, 2 * R + r, :], y3s[(nb, ch, r)], 3, r)
+                merge(by_n(pl[:, 2 * R + r, :]), bank_by_n(y3s[(nb, ch, r)]), 3, r)
             elif ch == 2:
-                merge(pl[:, 2 * R + r, :128], y3s[(nb, ch, r)], 3, r)
+                merge(by_n(pl[:, 2 * R + r, :])[:, :, 0:4], bank_by_n(y3s[(nb, ch, r)]), 3, r)
 
         with tc.tile_pool(name="stage", bufs=1) as stage:
             xraw = {}
@@ -275,7 +291,9 @@ def tile_bertheading_pa_kernel(tc, words_emb, W1, b1, W2, b2, W3, b3, out_0, out
                 chunk[(nb, ch)] = (sq_t, ns_t)
             sq, ns = chunk[(nb, ch)]
             nc.scalar.activation(out=sq[:, r, :t], in_=code[:, r, col0 : col0 + t], func=ACT.Square)
-            nc.tensor.matmul(out=ns[:, :t], lhsT=ones[:], rhs=sq[:, r, :t], start=(r == 0), stop=(r == R - 1))
+            if r % 2 == 1:
+                nc.gpsimd.tensor_tensor(out=sq[:, r, :t], in0=sq[:, r, :t], in1=sq[:, r - 1, :t], op=ALU.add)
+                nc.tensor.matmul(out=ns[:, :t], lhsT=ones[:], rhs=sq[:, r, :t], start=(r == 1), stop=(r == R - 1))
 
         def finish_chunk(nb, ch):
             code = half[nb][0]
@@ -288,7 +306,7 @@ def tile_bertheading_pa_kernel(tc, words_emb, W1, b1, W2, b2, W3, b3, out_0, out
             rn = late.tile([P, 512], F32, tag="rn", name="rn")
             nc.scalar.activation(
                 out=rn[:, :t].rearrange("m (n p) -> m n p", n=NH),
-                in_=ns[:, :t].rearrange("m (p n) -> m n p", n=NH),
+                in_=ns[:, :t].rearrange("m (p n) -> m n p" if ch == 2 else "m (n p) -> m n p", n=NH),
                 func=ACT.Relu,
                 bias=negeps[:],
                 scale=1.0,
@@ -301,9 +319,11 @@ def tile_bertheading_pa_kernel(tc, words_emb, W1, b1, W2, b2, W3, b3, out_0, out
                 part = (q * w) // (NH // 2)
                 outt = half[(nb, "out")][part]
                 osl = slice(q * w - part * (NH // 2), (q + 1) * w - part * (NH // 2))
-                nc.vector.tensor_tensor(
+                nc.gpsimd.tensor_tensor(
                     out=outt[:].rearrange("m n (r p) -> m n r p", r=R)[:, osl, :, p0 : p0 + npos],
-                    in0=code[:, :, col0 : col0 + t].rearrange("m r (p n) -> m n r p", n=NH)[:, nsl, :, :],
+                    in0=code[:, :, col0 : col0 + t].rearrange(
+                        "m r (p n) -> m n r p" if ch == 2 else "m r (n p) -> m n r p", n=NH
+                    )[:, nsl, :, :],
                     in1=rn[:, :t]
                     .rearrange("m (n p) -> m n p", n=NH)[:, nsl, :]
                     .unsqueeze(2)
@@ -316,11 +336,16 @@ def tile_bertheading_pa_kernel(tc, words_emb, W1, b1, W2, b2, W3, b3, out_0, out
 
         def trees(nb):
             pl = half[nb][1]
-            for w in (256, 128, 64):
-                vmax(pl[:, :, :w], pl[:, :, :w], pl[:, :, w : 2 * w])
+            pm = late.tile([P, 3 * R, NH], F32, tag="pm", name="pm")
+            nc.vector.tensor_reduce(
+                out=pm[:].rearrange("m g n -> m (g n)"),
+                in_=pl[:].rearrange("m g (n p) -> m (g n) p", n=NH),
+                axis=mybir.AxisListType.X,
+                op=ALU.max,
+            )
             ph = pt[:, :, nb * NH : (nb + 1) * NH]
-            nc.vector.tensor_tensor(out=ph, in0=pl[:, 0:R, :NH], in1=pl[:, R : 2 * R, :NH], op=ALU.add)
-            nc.vector.tensor_tensor(out=ph, in0=ph, in1=pl[:, 2 * R : 3 * R, :NH], op=ALU.add)
+            nc.vector.tensor_tensor(out=ph, in0=pm[:, 0:R, :], in1=pm[:, R : 2 * R, :], op=ALU.add)
+            nc.vector.tensor_tensor(out=ph, in0=ph, in1=pm[:, 2 * R : 3 * R, :], op=ALU.add)
 
         items = [(3, 0, ch, r) for ch in range(3) for r in range(R)]
         items += [(12, 1, r, ch) for r in range(R) for ch in range(3)]

@@ -319,7 +319,8 @@ def tile_bertheading_pa_kernel(tc, words_emb, W1, b1, W2, b2, W3, b3, out_0, out
                 part = (q * w) // (NH // 2)
                 outt = half[(nb, "out")][part]
                 osl = slice(q * w - part * (NH // 2), (q + 1) * w - part * (NH // 2))
-                nc.gpsimd.tensor_tensor(
+                eng = nc.vector if nb == 1 else nc.gpsimd
+                eng.tensor_tensor(
                     out=outt[:].rearrange("m n (r p) -> m n r p", r=R)[:, osl, :, p0 : p0 + npos],
                     in0=code[:, :, col0 : col0 + t].rearrange(
                         "m r (p n) -> m n r p" if ch == 2 else "m r (n p) -> m n r p", n=NH
@@ -337,12 +338,13 @@ def tile_bertheading_pa_kernel(tc, words_emb, W1, b1, W2, b2, W3, b3, out_0, out
         def trees(nb):
             pl = half[nb][1]
             pm = late.tile([P, 3 * R, NH], F32, tag="pm", name="pm")
-            nc.vector.tensor_reduce(
-                out=pm[:].rearrange("m g n -> m (g n)"),
-                in_=pl[:].rearrange("m g (n p) -> m (g n) p", n=NH),
-                axis=mybir.AxisListType.X,
-                op=ALU.max,
-            )
+            for k in range(3):
+                nc.vector.tensor_reduce(
+                    out=pm[:, R * k : R * (k + 1), :].rearrange("m g n -> m (g n)"),
+                    in_=pl[:, R * k : R * (k + 1), :].rearrange("m g (n p) -> m (g n) p", n=NH),
+                    axis=mybir.AxisListType.X,
+                    op=ALU.max,
+                )
             ph = pt[:, :, nb * NH : (nb + 1) * NH]
             nc.vector.tensor_tensor(out=ph, in0=pm[:, 0:R, :], in1=pm[:, R : 2 * R, :], op=ALU.add)
             nc.vector.tensor_tensor(out=ph, in0=ph, in1=pm[:, 2 * R : 3 * R, :], op=ALU.add)

@@ -31,11 +31,12 @@ def tile_bertheading_pa_kernel(tc, words_emb, W1, b1, W2, b2, W3, b3, out_0, out
     with ExitStack() as ctx:
         keep = ctx.enter_context(tc.tile_pool(name="keep", bufs=1))
         main = ctx.enter_context(tc.tile_pool(name="main", bufs=2))
-        psum_y = ctx.enter_context(tc.psum_pool(name="psum_y", bufs=6))
-        psum_aux = ctx.enter_context(tc.psum_pool(name="psum_aux", bufs=2))
+        psum_y = ctx.enter_context(tc.psum_pool(name="psum_y", bufs=7))
+        psum_aux = ctx.enter_context(tc.psum_pool(name="psum_aux", bufs=1))
 
         ident = keep.tile([P, P], F32, name="ident")
         make_identity(nc, ident[:])
+        ctx.enter_context(tc.manual_schedule())
 
         ones = keep.tile([P, P], F32, name="ones")
         nc.vector.memset(ones[:], 1.0)
@@ -111,13 +112,12 @@ def tile_bertheading_pa_kernel(tc, words_emb, W1, b1, W2, b2, W3, b3, out_0, out
             cd = code[:, r, col0 : col0 + t]
             if ch == 0:
                 y1 = conv_group(1, nb, r, 0, 8)
-                y1d = conv_group(1, nb, r, 0, 8)
                 y2 = conv_group(2, nb, r, 0, 8)
                 relu_out(by_n(pl[:, r, :]), bank_by_n(y1[:]), 1, r)
                 relu_out(by_n(pl[:, R + r, :]), bank_by_n(y2[:]), 2, r)
                 nc.vector.scalar_tensor_tensor(
                     out=by_n(cd),
-                    in0=bank_by_n(y1d[:]),
+                    in0=bank_by_n(y1[:]),
                     scalar=bias[:, 0, r : r + 1],
                     in1=by_n(pl[:, R + r, :]),
                     op0=ALU.add,
@@ -125,19 +125,17 @@ def tile_bertheading_pa_kernel(tc, words_emb, W1, b1, W2, b2, W3, b3, out_0, out
                 )
             elif ch == 1:
                 y1 = conv_group(1, nb, r, 8, 8)
-                y1d = conv_group(1, nb, r, 8, 8)
                 y2 = conv_group(2, nb, r, 8, 8)
                 relu_out(by_n(cd), bank_by_n(y1[:]), 1, r)
-                merge(by_n(pl[:, r, :]), bank_by_n(y1d[:]), 1, r)
                 merge(by_n(cd), bank_by_n(y2[:]), 2, r)
+                merge(by_n(pl[:, r, :]), bank_by_n(y1[:]), 1, r)
                 merge(by_n(pl[:, R + r, :]), bank_by_n(y2[:]), 2, r)
             else:
                 y1 = conv_group(1, nb, r, 16, 4)
-                y1d = conv_group(1, nb, r, 16, 4)
                 y2 = conv_group(2, nb, r, 15, 4)
                 relu_out(cd, y1[:, :256], 1, r)
-                merge(by_n(pl[:, r, :])[:, :, 0:4], bank_by_n(y1d[:, :256]), 1, r)
                 merge(code[:, r, col0 : col0 + 192], y2[:, 64:256], 2, r)
+                merge(by_n(pl[:, r, :])[:, :, 0:4], bank_by_n(y1[:, :256]), 1, r)
                 merge(by_n(pl[:, R + r, :])[:, :, 0:4], bank_by_n(y2[:, :256]), 2, r)
 
         y3s = {}
@@ -286,13 +284,18 @@ def tile_bertheading_pa_kernel(tc, words_emb, W1, b1, W2, b2, W3, b3, out_0, out
             code = half[nb][0]
             col0, t, p0, npos = CH[ch]
             if r == 0:
-                sq_t = late.tile([P, R, 512], F32, tag="sq", name="sq")
-                ns_t = psum_aux.tile([P, 512], F32, tag="aux", name="ns")
-                chunk[(nb, ch)] = (sq_t, ns_t)
-            sq, ns = chunk[(nb, ch)]
+                chunk[(nb, ch, "sq")] = late.tile([P, R, 512], F32, tag="sq", name="sq")
+            sq = chunk[(nb, ch, "sq")]
             nc.scalar.activation(out=sq[:, r, :t], in_=code[:, r, col0 : col0 + t], func=ACT.Square)
             if r % 2 == 1:
                 nc.gpsimd.tensor_tensor(out=sq[:, r, :t], in0=sq[:, r, :t], in1=sq[:, r - 1, :t], op=ALU.add)
+
+        def norm_mm(nb, ch):
+            t = CH[ch][1]
+            sq = chunk[(nb, ch, "sq")]
+            ns = psum_aux.tile([P, 512], F32, tag="aux", name="ns")
+            chunk[(nb, ch)] = (sq, ns)
+            for r in (1, 3):
                 nc.tensor.matmul(out=ns[:, :t], lhsT=ones[:], rhs=sq[:, r, :t], start=(r == 1), stop=(r == R - 1))
 
         def finish_chunk(nb, ch):
@@ -319,8 +322,7 @@ def tile_bertheading_pa_kernel(tc, words_emb, W1, b1, W2, b2, W3, b3, out_0, out
                 part = (q * w) // (NH // 2)
                 outt = half[(nb, "out")][part]
                 osl = slice(q * w - part * (NH // 2), (q + 1) * w - part * (NH // 2))
-                eng = nc.vector if nb == 1 else nc.gpsimd
-                eng.tensor_tensor(
+                nc.gpsimd.tensor_tensor(
                     out=outt[:].rearrange("m n (r p) -> m n r p", r=R)[:, osl, :, p0 : p0 + npos],
                     in0=code[:, :, col0 : col0 + t].rearrange(
                         "m r (p n) -> m n r p" if ch == 2 else "m r (n p) -> m n r p", n=NH
@@ -354,31 +356,34 @@ def tile_bertheading_pa_kernel(tc, words_emb, W1, b1, W2, b2, W3, b3, out_0, out
         items += [(3, 1, ch, r) for ch in range(3) for r in range(R)]
         pending = []
         n_items = len(items)
-        for i in range(n_items + LAG + 2):
+        for i in range(n_items + 9):
             if i < n_items:
                 kind, nb, a, b = items[i]
                 if kind == 12:
                     k12(nb, a, b)
                 else:
-                    lag = LAG if nb == 0 else 2
                     k3_code(nb, a, b)
                     if nb == 0:
                         k3_pool(nb, a, b)
-                    pending.append((i + lag, 0, nb, a, b))
+                    pending.append((i + 3, 0, nb, a, b))
                     if b == R - 1:
-                        pending.append((i + lag + 1, 1, nb, a, b))
+                        pending.append((i + 6, 1, nb, a, b))
+                        pending.append((i + 8, 2, nb, a, b))
+            if i == n_items - 1:
+                for ch in (1, 2):
+                    for r in range(R):
+                        k3_pool(1, ch, r)
+                trees(0)
+                trees(1)
             due = [e for e in pending if e[0] <= i]
             pending = [e for e in pending if e[0] > i]
             for e in due:
                 if e[1] == 0:
                     norm_part(e[2], e[3], e[4])
+                elif e[1] == 1:
+                    norm_mm(e[2], e[3])
                 else:
                     finish_chunk(e[2], e[3])
-        for ch in (1, 2):
-            for r in range(R):
-                k3_pool(1, ch, r)
-        trees(0)
-        trees(1)
 
         ptp = psum_aux.tile([P, R, P], F32, tag="aux", name="ptp")
         for r in range(R):

@@ -36,7 +36,6 @@ def tile_bertheading_pa_kernel(tc, words_emb, W1, b1, W2, b2, W3, b3, out_0, out
 
         ident = keep.tile([P, P], F32, name="ident")
         make_identity(nc, ident[:])
-        ctx.enter_context(tc.manual_schedule())
 
         ones = keep.tile([P, P], F32, name="ones")
         nc.vector.memset(ones[:], 1.0)
@@ -112,12 +111,13 @@ def tile_bertheading_pa_kernel(tc, words_emb, W1, b1, W2, b2, W3, b3, out_0, out
             cd = code[:, r, col0 : col0 + t]
             if ch == 0:
                 y1 = conv_group(1, nb, r, 0, 8)
+                y1d = conv_group(1, nb, r, 0, 8)
                 y2 = conv_group(2, nb, r, 0, 8)
                 relu_out(by_n(pl[:, r, :]), bank_by_n(y1[:]), 1, r)
                 relu_out(by_n(pl[:, R + r, :]), bank_by_n(y2[:]), 2, r)
                 nc.vector.scalar_tensor_tensor(
                     out=by_n(cd),
-                    in0=bank_by_n(y1[:]),
+                    in0=bank_by_n(y1d[:]),
                     scalar=bias[:, 0, r : r + 1],
                     in1=by_n(pl[:, R + r, :]),
                     op0=ALU.add,
@@ -125,17 +125,19 @@ def tile_bertheading_pa_kernel(tc, words_emb, W1, b1, W2, b2, W3, b3, out_0, out
                 )
             elif ch == 1:
                 y1 = conv_group(1, nb, r, 8, 8)
+                y1d = conv_group(1, nb, r, 8, 8)
                 y2 = conv_group(2, nb, r, 8, 8)
                 relu_out(by_n(cd), bank_by_n(y1[:]), 1, r)
+                merge(by_n(pl[:, r, :]), bank_by_n(y1d[:]), 1, r)
                 merge(by_n(cd), bank_by_n(y2[:]), 2, r)
-                merge(by_n(pl[:, r, :]), bank_by_n(y1[:]), 1, r)
                 merge(by_n(pl[:, R + r, :]), bank_by_n(y2[:]), 2, r)
             else:
                 y1 = conv_group(1, nb, r, 16, 4)
+                y1d = conv_group(1, nb, r, 16, 4)
                 y2 = conv_group(2, nb, r, 15, 4)
                 relu_out(cd, y1[:, :256], 1, r)
+                merge(by_n(pl[:, r, :])[:, :, 0:4], bank_by_n(y1d[:, :256]), 1, r)
                 merge(code[:, r, col0 : col0 + 192], y2[:, 64:256], 2, r)
-                merge(by_n(pl[:, r, :])[:, :, 0:4], bank_by_n(y1[:, :256]), 1, r)
                 merge(by_n(pl[:, R + r, :])[:, :, 0:4], bank_by_n(y2[:, :256]), 2, r)
 
         y3s = {}
@@ -284,18 +286,13 @@ def tile_bertheading_pa_kernel(tc, words_emb, W1, b1, W2, b2, W3, b3, out_0, out
             code = half[nb][0]
             col0, t, p0, npos = CH[ch]
             if r == 0:
-                chunk[(nb, ch, "sq")] = late.tile([P, R, 512], F32, tag="sq", name="sq")
-            sq = chunk[(nb, ch, "sq")]
+                sq_t = late.tile([P, R, 512], F32, tag="sq", name="sq")
+                ns_t = psum_aux.tile([P, 512], F32, tag="aux", name="ns")
+                chunk[(nb, ch)] = (sq_t, ns_t)
+            sq, ns = chunk[(nb, ch)]
             nc.scalar.activation(out=sq[:, r, :t], in_=code[:, r, col0 : col0 + t], func=ACT.Square)
             if r % 2 == 1:
                 nc.gpsimd.tensor_tensor(out=sq[:, r, :t], in0=sq[:, r, :t], in1=sq[:, r - 1, :t], op=ALU.add)
-
-        def norm_mm(nb, ch):
-            t = CH[ch][1]
-            sq = chunk[(nb, ch, "sq")]
-            ns = psum_aux.tile([P, 512], F32, tag="aux", name="ns")
-            chunk[(nb, ch)] = (sq, ns)
-            for r in (1, 3):
                 nc.tensor.matmul(out=ns[:, :t], lhsT=ones[:], rhs=sq[:, r, :t], start=(r == 1), stop=(r == R - 1))
 
         def finish_chunk(nb, ch):
@@ -322,7 +319,8 @@ def tile_bertheading_pa_kernel(tc, words_emb, W1, b1, W2, b2, W3, b3, out_0, out
                 part = (q * w) // (NH // 2)
                 outt = half[(nb, "out")][part]
                 osl = slice(q * w - part * (NH // 2), (q + 1) * w - part * (NH // 2))
-                nc.gpsimd.tensor_tensor(
+                eng = nc.vector if nb == 1 else nc.gpsimd
+                eng.tensor_tensor(
                     out=outt[:].rearrange("m n (r p) -> m n r p", r=R)[:, osl, :, p0 : p0 + npos],
                     in0=code[:, :, col0 : col0 + t].rearrange(
                         "m r (p n) -> m n r p" if ch == 2 else "m r (n p) -> m n r p", n=NH
@@ -356,34 +354,31 @@ def tile_bertheading_pa_kernel(tc, words_emb, W1, b1, W2, b2, W3, b3, out_0, out
         items += [(3, 1, ch, r) for ch in range(3) for r in range(R)]
         pending = []
         n_items = len(items)
-        for i in range(n_items + 9):
+        for i in range(n_items + LAG + 2):
             if i < n_items:
                 kind, nb, a, b = items[i]
                 if kind == 12:
                     k12(nb, a, b)
                 else:
+                    lag = LAG if nb == 0 else 2
                     k3_code(nb, a, b)
                     if nb == 0:
                         k3_pool(nb, a, b)
-                    pending.append((i + 3, 0, nb, a, b))
+                    pending.append((i + lag, 0, nb, a, b))
                     if b == R - 1:
-                        pending.append((i + 6, 1, nb, a, b))
-                        pending.append((i + 8, 2, nb, a, b))
-            if i == n_items - 1:
-                for ch in (1, 2):
-                    for r in range(R):
-                        k3_pool(1, ch, r)
-                trees(0)
-                trees(1)
+                        pending.append((i + lag + 1, 1, nb, a, b))
             due = [e for e in pending if e[0] <= i]
             pending = [e for e in pending if e[0] > i]
             for e in due:
                 if e[1] == 0:
                     norm_part(e[2], e[3], e[4])
-                elif e[1] == 1:
-                    norm_mm(e[2], e[3])
                 else:
                     finish_chunk(e[2], e[3])
+        for ch in (1, 2):
+            for r in range(R):
+                k3_pool(1, ch, r)
+        trees(0)
+        trees(1)
 
         ptp = psum_aux.tile([P, R, P], F32, tag="aux", name="ptp")
         for r in range(R):

from contextlib import ExitStack

import concourse.mybir as mybir
from concourse.masks import make_identity

F32 = mybir.dt.float32
BF16 = mybir.dt.bfloat16
U32 = mybir.dt.uint32
U8 = mybir.dt.uint8
FP8X4 = mybir.dt.float8_e4m3fn_x4
ALU = mybir.AluOpType
ACT = mybir.ActivationFunctionType

P = 128
L = 20
D = 512
C = 512
NH = 64
HC = L * NH
R = 4
TAP0 = {1: 0, 2: 1, 3: 3}
CH = ((0, 512, 0, 8), (512, 512, 8, 8), (1024, 256, 16, 4))
LAG = 4
EPS2 = 1.0e-24

FLOPS = 2 * D * C * P * (20 + 2 * 19 + 3 * 18)


def tile_bertheading_pa_kernel(tc, words_emb, W1, b1, W2, b2, W3, b3, out_0, out_1):
    nc = tc.nc
    with ExitStack() as ctx:
        keep = ctx.enter_context(tc.tile_pool(name="keep", bufs=1))
        main = ctx.enter_context(tc.tile_pool(name="main", bufs=2))
        psum_y = ctx.enter_context(tc.psum_pool(name="psum_y", bufs=7))
        psum_aux = ctx.enter_context(tc.psum_pool(name="psum_aux", bufs=1))

        ident = keep.tile([P, P], F32, name="ident")
        make_identity(nc, ident[:])

        ones = keep.tile([P, P], F32, name="ones")
        nc.vector.memset(ones[:], 1.0)
        warm_in = keep.tile([P, 1], F32, name="warm_in")
        warm_out = keep.tile([P, 1], F32, name="warm_out")
        nc.vector.memset(warm_in[:], 1.0)
        negeps = keep.tile([P, 1], F32, name="negeps")
        nc.vector.memset(negeps[:], -EPS2)
        poseps = keep.tile([P, 1], F32, name="poseps")
        nc.vector.memset(poseps[:], EPS2)

        bias = keep.tile([P, 3, R], F32, name="bias")
        braws = []
        for k, b in enumerate((b1, b2, b3)):
            braw = keep.tile([P, R], BF16, name="braw%d" % k)
            nc.scalar.dma_start(out=braw[:], in_=b.rearrange("(m r) -> m r", r=R))
            braws.append(braw)
        nc.scalar.activation(out=warm_out[:], in_=warm_in[:], func=ACT.Abs_reciprocal_sqrt)

        xq = keep.tile([P, 2 * HC], U32, name="xq", align_bytes=64)
        xs = keep.tile([P, 2 * HC], U8, name="xs", align_bytes=64)
        wq = keep.tile([P, 6, C], U32, name="wq", align_bytes=64)
        ws = keep.tile([P, 6, C], U8, name="ws", align_bytes=64)
        pt = keep.tile([P, R, P], F32, name="pt")
        pooled = keep.tile([P, C], F32, name="pooled")

        half = {}
        chunk = {}
        for nb in range(2):
            code_t = main.tile([P, R, HC], F32, tag="code", name="code")
            pl_t = main.tile([P, 3 * R, 512], F32, tag="pl", name="pl")
            half[nb] = (code_t, pl_t)

        def conv_group(k, nb, r, p0, npos, bank=None):
            n = npos * NH
            y = bank
            if bank is None:
                y = psum_y.tile([P, 512], F32, tag="y", name="y")
            for j in range(k):
                tap = TAP0[k] + j
                c0 = nb * HC + (p0 + j) * NH
                nc.tensor.matmul_mx(
                    out=y[:, :n],
                    lhsT=wq[:, tap, r * P : (r + 1) * P].bitcast(FP8X4),
                    lhsT_scale=ws[:, tap, r * P : (r + 1) * P],
                    rhs=xq[:, c0 : c0 + n].bitcast(FP8X4),
                    rhs_scale=xs[:, c0 : c0 + n],
                    start=(j == 0),
                    stop=(j == k - 1),
                )
            return y

        def relu_out(dst, y, k, r):
            nc.scalar.activation(out=dst, in_=y, func=ACT.Relu, bias=bias[:, k - 1, r : r + 1], scale=1.0)

        def merge(dst, y, k, r):
            nc.vector.scalar_tensor_tensor(
                out=dst, in0=y, scalar=bias[:, k - 1, r : r + 1], in1=dst, op0=ALU.add, op1=ALU.max
            )

        def bank_by_n(ap):
            return ap.rearrange("m (p n) -> m n p", n=NH)

        def by_n(ap):
            return ap.rearrange("m (n p) -> m n p", n=NH)

        def vmax(dst, a, b):
            nc.vector.tensor_tensor(out=dst, in0=a, in1=b, op=ALU.max)

        def k12(nb, r, ch):
            code, pl = half[nb]
            col0, t, p0, npos = CH[ch]
            cd = code[:, r, col0 : col0 + t]
            if ch == 0:
                y1 = conv_group(1, nb, r, 0, 8)
                y1d = conv_group(1, nb, r, 0, 8)
                y2 = conv_group(2, nb, r, 0, 8)
                relu_out(by_n(pl[:, r, :]), bank_by_n(y1[:]), 1, r)
                relu_out(by_n(pl[:, R + r, :]), bank_by_n(y2[:]), 2, r)
                nc.vector.scalar_tensor_tensor(
                    out=by_n(cd),
                    in0=bank_by_n(y1d[:]),
                    scalar=bias[:, 0, r : r + 1],
                    in1=by_n(pl[:, R + r, :]),
                    op0=ALU.add,
                    op1=ALU.max,
                )
            elif ch == 1:
                y1 = conv_group(1, nb, r, 8, 8)
                y1d = conv_group(1, nb, r, 8, 8)
                y2 = conv_group(2, nb, r, 8, 8)
                relu_out(by_n(cd), bank_by_n(y1[:]), 1, r)
                merge(by_n(pl[:, r, :]), bank_by_n(y1d[:]), 1, r)
                merge(by_n(cd), bank_by_n(y2[:]), 2, r)
                merge(by_n(pl[:, R + r, :]), bank_by_n(y2[:]), 2, r)
            else:
                y1 = conv_group(1, nb, r, 16, 4)
                y1d = conv_group(1, nb, r, 16, 4)
                y2 = conv_group(2, nb, r, 15, 4)
                relu_out(cd, y1[:, :256], 1, r)
                merge(by_n(pl[:, r, :])[:, :, 0:4], bank_by_n(y1d[:, :256]), 1, r)
                merge(code[:, r, col0 : col0 + 192], y2[:, 64:256], 2, r)
                merge(by_n(pl[:, R + r, :])[:, :, 0:4], bank_by_n(y2[:, :256]), 2, r)

        y3s = {}

        def k3_code(nb, ch, r):
            code, pl = half[nb]
            col0, t, p0, npos = CH[ch]
            cd = code[:, r, col0 : col0 + t]
            if ch == 0:
                y3 = conv_group(3, nb, r, 0, 8)
                relu_out(by_n(pl[:, 2 * R + r, :]), bank_by_n(y3[:]), 3, r)
                vmax(cd, cd, pl[:, 2 * R + r, :])
            elif ch == 1:
                y3 = conv_group(3, nb, r, 8, 8)
                merge(by_n(cd), bank_by_n(y3[:]), 3, r)
                y3s[(nb, ch, r)] = y3[:]
            else:
                if r % 2 == 0:
                    y3s[nb] = psum_y.tile([P, 2, 256], F32, tag="y", name="y3c")
                y3 = y3s[nb][:, r % 2, :]
                conv_group(3, nb, r, 14, 4, bank=y3)
                merge(code[:, r, col0 : col0 + 128], y3[:, 128:256], 3, r)
                y3s[(nb, ch, r)] = y3

        def k3_pool(nb, ch, r):
            pl = half[nb][1]
            if ch == 1:
                merge(by_n(pl[:, 2 * R + r, :]), bank_by_n(y3s[(nb, ch, r)]), 3, r)
            elif ch == 2:
                merge(by_n(pl[:, 2 * R + r, :])[:, :, 0:4], bank_by_n(y3s[(nb, ch, r)]), 3, r)

        with tc.tile_pool(name="stage", bufs=1) as stage:
            xraw = {}
            wraw = {}
            wgs = {}
            taps = ((W1, 0), (W2, 0), (W2, 1), (W3, 0), (W3, 1), (W3, 2))

            def load_x(i):
                t = stage.tile([P, 4 * D], BF16, name="xraw%d" % i)
                nc.sync.dma_start(out=t[:], in_=words_emb[:, 4 * i : 4 * i + 4, :].rearrange("n p d -> n (p d)"))
                xraw[i] = t

            def load_w(tap):
                w, j = taps[tap]
                t = stage.tile([P, 4, C], BF16, name="wraw%d" % tap)
                nc.sync.dma_start(
                    out=t[:].rearrange("q (u e) c -> q u e c", u=2),
                    in_=w[j].rearrange("(u q e) c -> q u e c", u=2, e=2),
                )
                wraw[tap] = t

            load_w(0)
            load_x(0)
            load_x(1)
            load_w(1)
            load_x(2)
            load_w(2)
            load_x(3)
            load_x(4)
            load_w(3)
            load_w(4)
            load_w(5)

            xg = stage.tile([P, 2 * HC * 4], BF16, name="xg", align_bytes=64)
            xg32 = xg[:].bitcast(F32)

            def x_chunk(i):
                xw = xraw[i][:].bitcast(F32)
                for h in range(2):
                    xt = psum_y.tile([P, 2, 2, P], F32, tag="y", name="xt")
                    for pp in range(2):
                        for u in range(2):
                            w0 = (2 * h + pp) * 256 + u * 128
                            nc.tensor.transpose(xt[:, pp, u, :], xw[:, w0 : w0 + 128], ident[:])
                    pos = 4 * i + 2 * h
                    for nb in range(2):
                        f0 = (nb * HC + pos * NH) * 2
                        dst = xg32[:, f0 : f0 + 256].rearrange("q (pp n u) -> q pp n u", pp=2, u=2)
                        src = xt[:, :, :, nb * NH : (nb + 1) * NH].rearrange("q pp u n -> q pp n u")
                        nc.scalar.copy(out=dst, in_=src)

            def x_quant(c0, cols):
                nc.vector.quantize_mx(
                    out=xq[:, c0 : c0 + cols].bitcast(FP8X4),
                    scales=xs[:, c0 : c0 + cols],
                    in_=xg[:, 4 * c0 : 4 * (c0 + cols)],
                )

            def w_regroup(tap, on_vector):
                wg = stage.tile([P, C, 4], BF16, tag="wg", name="wg", bufs=3, align_bytes=64)
                dst = wg[:].rearrange("q (r m) t -> q r m t", r=R)
                src = wraw[tap][:].rearrange("q t (m r) -> q r m t", r=R)
                if on_vector:
                    nc.vector.tensor_copy(out=dst, in_=src)
                else:
                    nc.scalar.copy(out=dst, in_=src)
                wgs[tap] = wg

            def w_quant(tap):
                nc.vector.quantize_mx(
                    out=wq[:, tap, :].bitcast(FP8X4),
                    scales=ws[:, tap, :],
                    in_=wgs[tap][:].rearrange("q c t -> q (c t)"),
                )

            w_regroup(0, True)
            for k in range(3):
                nc.vector.tensor_copy(out=bias[:, k, :], in_=braws[k][:])
            x_chunk(0)
            x_chunk(1)
            w_quant(0)
            w_regroup(1, True)
            x_quant(0, 256)
            w_quant(1)
            x_chunk(2)
            x_quant(256, 256)
            w_regroup(2, True)
            x_quant(512, 256)
            w_quant(2)
            k12(0, 0, 0)
            x_chunk(3)
            x_chunk(4)
            x_quant(768, 256)
            x_quant(1024, 256)
            k12(0, 0, 1)
            k12(0, 0, 2)
            w_regroup(3, False)
            for ch in range(3):
                k12(0, 1, ch)
            w_regroup(4, False)
            w_quant(3)
            for ch in range(3):
                k12(0, 2, ch)
            w_regroup(5, True)
            w_quant(4)
            for ch in range(3):
                k12(0, 3, ch)
            w_quant(5)
            x_quant(HC, 1024)
            x_quant(HC + 1024, 256)

        late = ctx.enter_context(tc.tile_pool(name="late", bufs=2))
        o0v = out_0.rearrange("n (m r) p -> m n (r p)", r=R)

        def norm_part(nb, ch, r):
            code = half[nb][0]
            col0, t, p0, npos = CH[ch]
            if r == 0:
                sq_t = late.tile([P, R, 512], F32, tag="sq", name="sq")
                ns_t = psum_aux.tile([P, 512], F32, tag="aux", name="ns")
                chunk[(nb, ch)] = (sq_t, ns_t)
            sq, ns = chunk[(nb, ch)]
            nc.scalar.activation(out=sq[:, r, :t], in_=code[:, r, col0 : col0 + t], func=ACT.Square)
            if r % 2 == 1:
                nc.gpsimd.tensor_tensor(out=sq[:, r, :t], in0=sq[:, r, :t], in1=sq[:, r - 1, :t], op=ALU.add)
                nc.tensor.matmul(out=ns[:, :t], lhsT=ones[:], rhs=sq[:, r, :t], start=(r == 1), stop=(r == R - 1))

        def finish_chunk(nb, ch):
            code = half[nb][0]
            col0, t, p0, npos = CH[ch]
            ns = chunk[(nb, ch)][1]
            if ch == 0:
                outa_t = late.tile([P, NH // 2, R * L], F32, tag="outa", name="outa")
                outb_t = late.tile([P, NH // 2, R * L], F32, tag="outb", name="outb")
                half[(nb, "out")] = (outa_t, outb_t)
            rn = late.tile([P, 512], F32, tag="rn", name="rn")
            nc.scalar.activation(
                out=rn[:, :t].rearrange("m (n p) -> m n p", n=NH),
                in_=ns[:, :t].rearrange("m (p n) -> m n p" if ch == 2 else "m (n p) -> m n p", n=NH),
                func=ACT.Relu,
                bias=negeps[:],
                scale=1.0,
            )
            nc.scalar.activation(out=rn[:, :t], in_=rn[:, :t], func=ACT.Abs_reciprocal_sqrt, bias=poseps[:], scale=1.0)
            pieces = 4 if ch == 2 else 2
            w = NH // pieces
            for q in range(pieces):
                nsl = slice(q * w, (q + 1) * w)
                part = (q * w) // (NH // 2)
                outt = half[(nb, "out")][part]
                osl = slice(q * w - part * (NH // 2), (q + 1) * w - part * (NH // 2))
                eng = nc.vector if nb == 1 else nc.gpsimd
                eng.tensor_tensor(
                    out=outt[:].rearrange("m n (r p) -> m n r p", r=R)[:, osl, :, p0 : p0 + npos],
                    in0=code[:, :, col0 : col0 + t].rearrange(
                        "m r (p n) -> m n r p" if ch == 2 else "m r (n p) -> m n r p", n=NH
                    )[:, nsl, :, :],
                    in1=rn[:, :t]
                    .rearrange("m (n p) -> m n p", n=NH)[:, nsl, :]
                    .unsqueeze(2)
                    .to_broadcast([P, w, R, npos]),
                    op=ALU.mult,
                )
                if ch == 2:
                    n0 = nb * NH + q * w
                    nc.sync.dma_start(out=o0v[:, n0 : n0 + w, :], in_=outt[:, osl, :])

        def trees(nb):
            pl = half[nb][1]
            pm = late.tile([P, 3 * R, NH], F32, tag="pm", name="pm")
            for k in range(3):
                nc.vector.tensor_reduce(
                    out=pm[:, R * k : R * (k + 1), :].rearrange("m g n -> m (g n)"),
                    in_=pl[:, R * k : R * (k + 1), :].rearrange("m g (n p) -> m (g n) p", n=NH),
                    axis=mybir.AxisListType.X,
                    op=ALU.max,
                )
            ph = pt[:, :, nb * NH : (nb + 1) * NH]
            nc.vector.tensor_tensor(out=ph, in0=pm[:, 0:R, :], in1=pm[:, R : 2 * R, :], op=ALU.add)
            nc.vector.tensor_tensor(out=ph, in0=ph, in1=pm[:, 2 * R : 3 * R, :], op=ALU.add)

        items = [(3, 0, ch, r) for ch in range(3) for r in range(R)]
        items += [(12, 1, r, ch) for r in range(R) for ch in range(3)]
        items += [(3, 1, ch, r) for ch in range(3) for r in range(R)]
        pending = []
        n_items = len(items)
        for i in range(n_items + LAG + 2):
            if i < n_items:
                kind, nb, a, b = items[i]
                if kind == 12:
                    k12(nb, a, b)
                else:
                    lag = LAG if nb == 0 else 2
                    k3_code(nb, a, b)
                    if nb == 0:
                        k3_pool(nb, a, b)
                    pending.append((i + lag, 0, nb, a, b))
                    if b == R - 1:
                        pending.append((i + lag + 1, 1, nb, a, b))
            due = [e for e in pending if e[0] <= i]
            pending = [e for e in pending if e[0] > i]
            for e in due:
                if e[1] == 0:
                    norm_part(e[2], e[3], e[4])
                else:
                    finish_chunk(e[2], e[3])
        for ch in (1, 2):
            for r in range(R):
                k3_pool(1, ch, r)
        trees(0)
        trees(1)

        ptp = psum_aux.tile([P, R, P], F32, tag="aux", name="ptp")
        for r in range(R):
            nc.tensor.transpose(ptp[:, r, :], pt[:, r, :], ident[:])
        nc.scalar.activation(
            out=pooled[:].rearrange("n (m r) -> n m r", r=R),
            in_=ptp[:].rearrange("n r m -> n m r"),
            func=ACT.Copy,
            scale=1.0 / 3.0,
        )
        nc.sync.dma_start(out=out_1, in_=pooled[:])
